import numpy as np
import ml_dtypes


def mxq(x, axis, fmt="e4m3"):
    dtype, down = {"e4m3": (ml_dtypes.float8_e4m3fn, 7), "e5m2": (ml_dtypes.float8_e5m2, 14)}[fmt]
    v = np.moveaxis(np.asarray(x, np.float32).astype(ml_dtypes.bfloat16).astype(np.float64), axis, -1)
    blocks = v.reshape(v.shape[:-1] + (-1, 32))
    amax = np.abs(blocks).max(-1, keepdims=True)
    byte = np.maximum(np.where(amax > 0, np.frexp(amax)[1] - 1 + 127, 0) - down, 1)
    scale = np.exp2(byte - 127.0)
    codes = (blocks / scale).astype(np.float32).astype(dtype).astype(np.float64)
    return np.moveaxis((codes * scale).reshape(v.shape), -1, axis)


WIDE = False


def mx_kscale(k):
    if not WIDE:
        return np.ones(k)
    levels = np.array([18, -18])
    if k % 512:
        return np.exp2(np.random.permutation(np.resize(levels, k // 32))).repeat(32)
    a = np.empty((k // 512, 16))
    for p in range(k // 512):
        a[p, :8] = np.random.permutation(np.resize(levels, 8))
        for g in range(8):
            far = levels[np.abs(levels - a[p, g]) >= 10]
            a[p, g + 8] = far[np.random.randint(len(far))]
    return np.exp2(a.ravel()).repeat(32)


BF16 = ml_dtypes.bfloat16


def bf(x):
    return np.asarray(x, np.float32).astype(BF16)


def f64(x):
    return np.asarray(x).astype(np.float64)


B, HG, H, D, LSEQ, LK = 1, 40, 8, 128, 1024, 512
N = HG * HG
C = H * D
DILATIONS = (1, 2, 3)
POOL = 2


def landmarks(x):
    xg = f64(x).reshape(B, HG, HG, C)
    xm = np.concatenate([xg[:, ::d, ::d, :].reshape(B, -1, C) for d in DILATIONS], axis=1)
    return xm[:, :POOL * LSEQ].reshape(B, LSEQ, POOL, C).mean(axis=2)


def landmarks_back(dxl):
    sides = [len(range(0, HG, d)) for d in DILATIONS]
    dm = np.zeros((sum(r * r for r in sides), C))
    dm[:POOL * LSEQ] = np.repeat(dxl, POOL, axis=0) / POOL
    dg = np.zeros((HG, HG, C))
    start = 0
    for d, r in zip(DILATIONS, sides):
        dg[::d, ::d] += dm[start:start + r * r].reshape(r, r, C)
        start += r * r
    return dg.reshape(N, C)


def setup_inputs():
    u = mx_kscale(LK)
    v = mx_kscale(2 * C)
    s = mx_kscale(LSEQ)
    st = np.repeat(s[:N // POOL], POOL)
    se = np.where(np.arange(LSEQ) < N // POOL, s, np.max(s))
    x0 = bf(np.random.standard_normal((B, N, C)))
    W0 = bf(np.random.standard_normal((C, 2 * C)) * 1.6 / np.sqrt(C))
    b_kv = bf(np.random.standard_normal(2 * C) * 0.2)
    Ek0 = bf(np.random.standard_normal((LSEQ, LK)) / np.sqrt(LSEQ))
    Ev0 = bf(np.random.standard_normal((LSEQ, LK)) / np.sqrt(LSEQ))
    vk = v[:C].reshape(1, H, 1, D)
    vv = v[C:].reshape(1, H, 1, D)
    uj = u[None, None, :, None]
    grad_0 = bf(np.random.standard_normal((B, H, LK, D)) * np.exp2(np.random.randint(-6, 1, (B, 1, LK, 1))) * uj * vk)
    grad_1 = bf(np.random.standard_normal((B, H, LK, D)) * np.exp2(np.random.randint(-6, 1, (B, 1, LK, 1))) * uj * vv)
    kv = landmarks(x0) @ f64(W0) + f64(b_kv)
    return {"x": bf(f64(x0) * st[None, :, None]),
            "W_kv": bf(f64(W0) / v[None, :]),
            "b_kv": b_kv,
            "E_k": bf(f64(Ek0) / se[:, None] / u[None, :]),
            "E_v": bf(f64(Ev0) / se[:, None] / u[None, :]),
            "kv": np.asarray(kv, np.float32),
            "grad_0": grad_0,
            "grad_1": grad_1}


def reference(x, W_kv, b_kv, E_k, E_v, kv, grad_0, grad_1):
    g = np.stack([f64(t)[0].transpose(1, 0, 2).reshape(LK, C) for t in (grad_0, grad_1)])
    e = np.stack([f64(E_k), f64(E_v)])
    dh = mxq(e, 2, "e4m3") @ mxq(g, 1, "e5m2")
    dkv = np.concatenate([dh[0], dh[1]], axis=1)
    xl = landmarks(x)[0]
    dxl = mxq(dkv, 1, "e5m2") @ mxq(f64(W_kv), 1, "e4m3").T
    dW = mxq(xl, 0, "e4m3").T @ mxq(dkv, 0, "e5m2")
    dx = landmarks_back(dxl).reshape(B, N, C)
    return dx, dW

from contextlib import ExitStack

import concourse.mybir as mybir
from concourse.masks import make_identity

F32 = mybir.dt.float32
BF16 = mybir.dt.bfloat16
U32 = mybir.dt.uint32
I32 = mybir.dt.int32
U8 = mybir.dt.uint8
E4X4 = mybir.dt.float8_e4m3fn_x4
E5X4 = mybir.dt.float8_e5m2_x4
COPY = mybir.ActivationFunctionType.Copy
ADD = mybir.AluOpType.add
MULT = mybir.AluOpType.mult

FLOPS = 2 * 1024 * 512 * 2048 + 2 * 1024 * 2048 * 1024 + 2 * 1024 * 1024 * 2048
BYTES = 2 * (1600 * 1024 + 1024 * 2048 + 2 * 1024 * 512 + 2 * 512 * 1024) + 4 * (1600 * 1024 + 1024 * 2048)

LOADS = "G00 G01 E00 E01 L5 E11 W1 L9 L4 X1 L1 W2 L11 L2 G10 L0 W3 E10 G11 L10 L8 L6 W0 L7 L3 X0 L12".split()

ORDER = [
    ("XZ",),
    ("G", 1, 0),
    ("G", 0, 1),
    ("E", 0, 0, 0),
    ("E", 0, 1, 0),
    ("E", 1, 1, 2),
    ("D", 0, 1, 1, 1, 0),
    ("D", 0, 0, 0, 0, 3),
    ("D", 1, 0, 3, 0, 3),
    ("D", 1, 1, 3, 0, 2),
    ("X", 1, 1),
    ("W", 1, 1, 0),
    ("E", 1, 0, 0),
    ("G", 3, 0),
    ("G", 2, 1),
    ("W", 3, 1, 0),
    ("X", 0, 1),
    ("W", 3, 0, 0),
    ("W", 0, 0, 0),
    ("D", 3, 0, 0, 0, 0),
    ("W", 1, 0, 1),
    ("D", 2, 0, 0, 1, 3),
    ("DW", 5, 0, 2),
    ("W", 2, 0, 1),
    ("W", 0, 1, 0),
    ("W", 2, 1, 1),
    ("X", 1, 0),
    ("D", 2, 1, 0, 2, 4),
    ("DX", 0, 3, 0),
    ("DX", 0, 0, 0),
    ("DX", 0, 2, 0),
    ("X", 0, 0),
    ("DX", 0, 1, 1),
    ("DW", 3, 0, 0),
    ("DW", 2, 0, 1),
    ("DW", 0, 0, 0),
    ("D", 3, 1, 2, 1, 2),
    ("DW", 7, 0, 2),
    ("XR", 0),
    ("DW", 6, 0, 0),
    ("DW", 1, 0, 0),
    ("FIN", 0, 1),
    ("FIN", 0, 0),
    ("FIN", 0, 2),
    ("FIN", 0, 3),
    ("DW", 0, 1, 0),
    ("DW", 3, 1, 0),
    ("DX", 1, 1, 1),
    ("DX", 1, 2, 1),
    ("DW", 5, 1, 1),
    ("XR", 1),
    ("DW", 1, 1, 2),
    ("DW", 2, 1, 0),
    ("FIN", 1, 2),
    ("DX", 1, 0, 1),
    ("FIN", 1, 1),
    ("L3",),
    ("DW", 6, 1, 0),
    ("DW", 4, 0, 0),
    ("FIN", 1, 0),
    ("DW", 4, 1, 2),
    ("DX", 1, 3, 2),
    ("FIN", 1, 3),
    ("DW", 7, 1, 2),
]

NA = 72


def tile_efficientmultiscaledilatedattention_pa_v_kernel(tc, x, W_kv, b_kv, E_k, E_v, kv, grad_0, grad_1, out_0, out_1):
    nc = tc.nc
    with ExitStack() as ctx:
        const = ctx.enter_context(tc.tile_pool(name="const", bufs=1))
        pool = ctx.enter_context(tc.tile_pool(name="pool", bufs=1))
        psum = ctx.enter_context(tc.psum_pool(name="psum", bufs=1))

        ctx.enter_context(tc.manual_schedule())
        ident = const.tile([128, 128], F32, name="ident", align_bytes=64)
        make_identity(nc, ident[:])

        def r8(name, shape, dt):
            return pool.tile(shape, dt, name=name, tag="r8", bufs=6, align_bytes=64)

        def p4(name):
            return pool.tile([128, 2048], BF16, name=name, tag="p4", bufs=6, align_bytes=64)

        def codes(name, tag, bufs):
            c = pool.tile([128, 1024], U32, name=name + "c", tag=tag + "c", bufs=bufs, align_bytes=64)
            s = pool.tile([128, 1024], U8, name=name + "s", tag=tag + "s", bufs=bufs, align_bytes=64)
            return c, s

        def quant(cs, a, fmt, src):
            c, s = cs
            nc.vector.quantize_mx(out=c[:, a:a + 512].bitcast(fmt), scales=s[:, a:a + 512], in_=src[:])

        xf = x[0]
        raw_e = [None, None]
        raw_g = [None, None]
        e_src = [E_k, E_v]
        g_src = [grad_0[0], grad_1[0]]

        def load_e(e, grp):
            t = raw_e[e]
            if grp == 1:
                nc.sync.dma_start(out=t[:, 4:8, :], in_=e_src[e][288:800, :].rearrange("(p t) k -> p t k", t=4))
            else:
                nc.sync.dma_start(out=t[0:NA, 0:4, :], in_=e_src[e][0:288, :].rearrange("(p t) k -> p t k", t=4))
                nc.sync.dma_start(out=t[NA:128, 0:4, :], in_=e_src[e][800:1024, :].rearrange("(p t) k -> p t k", t=4))

        def load_g(e, b):
            nc.sync.dma_start(out=raw_g[e][:, 4 * b:4 * b + 4, :],
                              in_=g_src[e][4 * b:4 * b + 4].rearrange("h (p j) d -> p h (j d)", j=4))

        raw_x = {}
        raw_x[1] = pool.tile([128, 8, 1024], BF16, name="xB", tag="x16", bufs=2, align_bytes=64)
        raw_x[0] = pool.tile([128, 8, 1024], BF16, name="xA", tag="x16", bufs=2, align_bytes=64)
        xa = raw_x[0]
        two = xf.rearrange("(a n) c -> a n c", n=160)
        three = xf[0:378, :].rearrange("(a n) c -> a n c", n=126)
        row3 = xf[0:480, :].rearrange("(n three) c -> n three c", three=3)
        q0 = NA + 50
        SECOND = ((0, 0, 8, 0), (1, 0, 8, 16), (2, 0, 4, 32), (2, 4, 8, 80), (3, 0, 8, 88), (4, 0, 8, 104))
        THIRD = ((0, 6, 0, 8, 0, 3, 0), (1, 6, 0, 2, 0, 3, 24), (1, 6, 6, 8, 0, 3, 120), (1, 4, 2, 4, 0, 2, 30), (3, 6, 4, 6, 1, 3, 114))

        def load_list(i):
            if i < 6:
                b, s0, s1, n0 = SECOND[i]
                nc.sync.dma_start(out=xa[NA + b:NA + 50:5, s0:s1, :], in_=two[:, n0:n0 + 2 * (s1 - s0):2, :])
            elif i < 11:
                ps, pe, s0, s1, a0, a1, n0 = THIRD[i - 6]
                nc.sync.dma_start(out=xa[q0 + ps:q0 + pe:2, s0:s1, :], in_=three[a0:a1, n0:n0 + 3 * (s1 - s0):3, :])
            elif i == 11:
                nc.sync.dma_start(out=xa[q0 + 5:q0 + 6, 2:4, :], in_=row3[120:122, 0:1, :].rearrange("n o c -> o n c"))
            else:
                nc.sync.dma_start(out=xa[q0 + 1:q0 + 2, 4:6, :], in_=row3[12:14, 0:1, :].rearrange("n o c -> o n c"))

        raw_w = [None] * 4

        def load(tok):
            kind, i = tok[0], tok[1:]
            if kind == "L":
                load_list(int(i))
            elif kind == "E":
                if raw_e[int(i[0])] is None:
                    raw_e[int(i[0])] = r8("e" + i[0], [128, 8, 512], BF16)
                load_e(int(i[0]), int(i[1]))
            elif kind == "G":
                if raw_g[int(i[0])] is None:
                    raw_g[int(i[0])] = r8("g" + i[0], [128, 8, 512], BF16)
                load_g(int(i[0]), int(i[1]))
            elif kind == "W":
                w = raw_w[int(i)] = r8("w" + i, [128, 2, 2048], BF16)
                nc.sync.dma_start(out=w[:], in_=W_kv[256 * int(i):256 * int(i) + 256, :].rearrange("(n p) f -> p n f", p=128))
            elif i == "1":
                nc.sync.dma_start(out=raw_x[1][:], in_=xf[576:1600, :].rearrange("(p j) c -> p j c", j=8))
            else:
                nc.sync.dma_start(out=xa[0:NA], in_=xf[0:576, :].rearrange("(p j) c -> p j c", j=8))

        for tok in LOADS:
            load(tok)

        ec = [codes("ek", "e", 2), codes("ev", "e", 2)]
        gc = [codes("g0", "g", 2), codes("g1", "g", 2)]
        xc = [codes("xa", "x", 2), codes("xb", "x", 2)]
        wc = [codes("w%d" % i, "w", 4) for i in range(4)]
        tcod = [codes("t%d" % i, "t", 4) for i in range(4)]
        dc = {}

        def bank(name):
            return psum.tile([128, 512], F32, name=name, tag="ps", bufs=8)

        def evict(on_dve, dst, src):
            if on_dve:
                nc.vector.tensor_copy(out=dst, in_=src)
            else:
                nc.scalar.copy(out=dst, in_=src)

        def flips(words_of, dst4, dve):
            outs = []
            for h in range(2):
                ps = bank("pst")
                v = ps[:].rearrange("p (t u c) -> p t u c", t=2, u=2)
                for t in range(2):
                    for u in range(2):
                        nc.tensor.transpose(v[:, t, u, :], words_of(2 * h + t, u), ident[:])
                outs.append(v.rearrange("p t u c -> p t c u"))

            def copies():
                for h in range(2):
                    evict(dve > h, dst4[:, 2 * h:2 * h + 2], outs[h])
            return copies

        def quads(pre):
            return pre[:].bitcast(F32).rearrange("p (t c u) -> p t c u", t=4, u=2)

        def e_job(e, grp, dve=0):
            box = {}

            def s0():
                words = raw_e[e][:].bitcast(F32)
                box["p"] = p4("epre")
                box["c"] = flips(lambda t, u: words[:, 4 * grp + t, u:256:2], quads(box["p"]), dve)
            return [s0, lambda: box["c"](), lambda: quant(ec[e], 512 * grp, E4X4, box["p"])]

        def g_job(fb, act=0):
            e, b = divmod(fb, 2)
            box = {}

            def s1():
                pre = box["p"] = p4("gpre")
                src = raw_g[e][:, 4 * b:4 * b + 4, :].rearrange("p h (j d) -> p h d j", j=4)
                dst = pre[:].rearrange("p (h d j) -> p h d j", h=4, j=4)
                if act:
                    nc.scalar.copy(out=dst, in_=src)
                else:
                    nc.vector.tensor_copy(out=dst, in_=src)
            return [lambda: None, s1, lambda: quant(gc[e], 512 * b, E5X4, box["p"])]

        def d_job(fb, grp, dve=0, tdve=0, iact=0):
            e, b = divmod(fb, 2)
            box = {}

            def s0():
                if fb not in dc:
                    dc[fb] = codes("d%d" % fb, "d", 4)
                box["ps"] = []
                for t in range(4):
                    ps = bank("psd")
                    a = 512 * grp + 128 * t
                    nc.tensor.matmul_mx(
                        out=ps[:], lhsT=ec[e][0][:, a:a + 128].bitcast(E4X4), lhsT_scale=ec[e][1][:, a:a + 128],
                        rhs=gc[e][0][:, 512 * b:512 * b + 512].bitcast(E5X4), rhs_scale=gc[e][1][:, 512 * b:512 * b + 512],
                        start=True, stop=True)
                    box["ps"].append(ps)

            def s1():
                d = box["d"] = pool.tile([128, 4, 512], BF16, name="dsb", tag="dsb", bufs=3, align_bytes=64)
                for t in range(4):
                    src = box["ps"][t][:].rearrange("p (m u e) -> p u m e", u=2, e=2)
                    dst = d[:, t, :].rearrange("p (u m e) -> p u m e", u=2, e=2)
                    if t >= 4 - dve:
                        nc.vector.tensor_scalar(out=dst, in0=src, scalar1=0.5, scalar2=None, op0=MULT)
                    else:
                        nc.scalar.activation(out=dst, in_=src, func=COPY, scale=0.5)

            def s2():
                words = box["d"][:].bitcast(F32)
                box["tp"] = p4("tpre")
                box["c"] = flips(lambda t, u: words[:, t, 128 * u:128 * u + 128], quads(box["tp"]), tdve)
                pre = box["dp"] = p4("dpre")
                pv = pre[:].rearrange("p (f t) -> p f t", t=4)
                dv = box["d"][:].rearrange("p t f -> p f t")
                if iact < 4:
                    nc.vector.tensor_copy(out=pv[:, 128 * iact:, :], in_=dv[:, 128 * iact:, :])
                if iact > 0:
                    nc.scalar.copy(out=pv[:, 0:128 * iact, :], in_=dv[:, 0:128 * iact, :])

            def s3():
                box["c"]()
                quant(dc[fb], 512 * grp, E5X4, box["dp"])
            return [s0, s1, s2, s3, lambda: quant(tcod[fb], 512 * grp, E5X4, box["tp"])]

        def x_job(grp, h):
            box = {}

            def s1():
                v = raw_x[grp][:].rearrange("p (t two) c -> p two c t", two=2)
                pre = box["p"] = p4("xpre")
                nc.vector.tensor_tensor(out=pre[:].rearrange("p (c t) -> p c t", t=4),
                                        in0=v[:, 0, 512 * h:512 * h + 512, :], in1=v[:, 1, 512 * h:512 * h + 512, :], op=ADD)
            return [lambda: None, s1, lambda: quant(xc[grp], 512 * h, E4X4, box["p"])]

        def w_job(fb, half, dve=0):
            box = {}

            def words_of(t, u):
                return raw_w[2 * half + t // 2][:].bitcast(F32)[:, t % 2, 256 * fb + u:256 * fb + 256:2]

            def s0():
                box["p"] = p4("wpre")
                box["c"] = flips(words_of, quads(box["p"]), dve)
            return [s0, lambda: box["c"](), lambda: quant(wc[fb], 512 * half, E4X4, box["p"])]

        def dw_job(n, pair, dve=0):
            box = {}

            def s0():
                box["ps"] = []
                for fb in (2 * pair, 2 * pair + 1):
                    ps = bank("psw")
                    for k, grp in enumerate((1, 0)):
                        nc.tensor.matmul_mx(
                            out=ps[:], lhsT=xc[grp][0][:, 128 * n:128 * n + 128].bitcast(E4X4), lhsT_scale=xc[grp][1][:, 128 * n:128 * n + 128],
                            rhs=dc[fb][0][:, 512 * grp:512 * grp + 512].bitcast(E5X4), rhs_scale=dc[fb][1][:, 512 * grp:512 * grp + 512],
                            start=(k == 0), stop=(k == 1))
                    box["ps"].append(ps)

            def s1():
                ob = box["o"] = pool.tile([128, 1024], F32, name="ob", tag="ob", bufs=4, align_bytes=64)
                for i in range(2):
                    evict(dve > i, ob[:, 512 * i:512 * i + 512].rearrange("p (m u e) -> p m u e", u=2, e=2),
                          box["ps"][i][:].rearrange("p (u m e) -> p m u e", u=2, e=2))

            def s2():
                nc.sync.dma_start(out=out_1[128 * n:128 * n + 128, 1024 * pair:1024 * pair + 1024], in_=box["o"][:])
            return [s0, s1, s2]

        of = out_0[0]
        parked = out_1[768:992, 1024:2048]
        ys = {}

        def dx_job(grp, t, dve=0):
            box = {}

            def s0():
                a = 512 * grp + 128 * t
                box["ps"] = []
                for h in range(2):
                    ps = bank("psx")
                    for fb in range(4):
                        nc.tensor.matmul_mx(
                            out=ps[:], lhsT=tcod[fb][0][:, a:a + 128].bitcast(E5X4), lhsT_scale=tcod[fb][1][:, a:a + 128],
                            rhs=wc[fb][0][:, 512 * h:512 * h + 512].bitcast(E4X4), rhs_scale=wc[fb][1][:, 512 * h:512 * h + 512],
                            start=(fb == 0), stop=(fb == 3))
                    box["ps"].append(ps)

            def s1():
                y = ys[(grp, t)] = r8("y", [128, 2, 1024], F32)
                for h in range(2):
                    evict(dve > h, y[:, 1, 512 * h:512 * h + 512], box["ps"][h][:])

            def s2():
                if grp == 0:
                    nc.sync.dma_start(out=parked.rearrange("(q t) c -> q t c", t=4)[:, t, :], in_=ys[(0, t)][NA:128, 1, :])
            return [s0, s1, s2]

        xt_box = []

        def xz_job():
            def s0():
                xt = pool.tile([128, 2, 2048], F32, name="xt", align_bytes=64)
                xt_box.append(xt)
                nc.vector.memset(xt[:].bitcast(I32), 0)
            return [s0]

        def xr_job(grp):
            def s0():
                xt = xt_box[0]
                pr = parked[0:200, :].rearrange("(r s) c -> r s c", s=10)
                for a in range(5):
                    if grp == 0:
                        r0, r1, p0, p1 = 0, (8 if a < 2 else 7), a, NA
                    else:
                        r0 = 8 if a < 2 else 7
                        r1, p0, p1 = 20, 10 * r0 + a - NA, 128
                    nc.sync.dma_start(out=xt[p0:p1:10, grp, :].rearrange("p (s c) -> p s c", s=2), in_=pr[r0:r1, 2 * a:2 * a + 2, :])
            return [s0]

        def fin_job(grp, t):
            def s0():
                y = ys[(grp, t)]
                b = t // 2
                nc.vector.tensor_tensor(out=y[:, 0, :], in0=y[:, 1, :], in1=xt_box[0][:, grp, 1024 * b:1024 * b + 1024], op=ADD)

            def s1():
                y = ys[(grp, t)]
                if grp == 0:
                    nc.sync.dma_start(out=of[0:576, :].rearrange("(p j) c -> p j c", j=8)[:, 2 * t:2 * t + 2, :], in_=y[0:NA])
                else:
                    nc.sync.dma_start(out=of[576:1600, :].rearrange("(p j) c -> p j c", j=8)[:, 2 * t:2 * t + 2, :], in_=y[:])
            return [s0, s1]

        def third_job():
            rows = of[0:480, :].rearrange("(r c three) k -> r c three k", r=4, three=3)
            box = {}

            def s0():
                z0 = box["a"] = pool.tile([128, 1024], F32, name="z0", tag="dsb", bufs=3, align_bytes=64)
                z1 = box["b"] = pool.tile([128, 1024], F32, name="z1", tag="dsb", bufs=3, align_bytes=64)
                for d in range(2):
                    nc.gpsimd.dma_start(out=z0[d:48:2, :], in_=parked[200:224, :])
                for r in range(4):
                    m = 14 if r < 3 else 6
                    nc.gpsimd.dma_start(out=z1[14 * r:14 * r + m, :], in_=rows[r, 0:m, 0, :])

            def s1():
                nc.vector.tensor_tensor(out=box["a"][0:48, :], in0=box["a"][0:48, :], in1=box["b"][0:48, :], op=ADD)

            def s2():
                for r in range(4):
                    m = 14 if r < 3 else 6
                    nc.gpsimd.dma_start(out=rows[r, 0:m, 0, :], in_=box["a"][14 * r:14 * r + m, :])
            return [s0, s1, s2]

        JOBS = {"E": e_job, "G": g_job, "D": d_job, "X": x_job, "W": w_job, "DW": dw_job, "DX": dx_job,
                "XZ": xz_job, "XR": xr_job, "FIN": fin_job, "L3": third_job}
        jobs = [JOBS[o[0]](*o[1:]) if o else [] for o in ORDER]
        depth = 5
        for i in range(len(jobs) + depth):
            for s in range(depth - 1, -1, -1):
                if 0 <= i - s < len(jobs) and s < len(jobs[i - s]):
                    jobs[i - s][s]()
